import numpy as np
import ml_dtypes

BF16 = ml_dtypes.bfloat16


def bf(x):
    return np.asarray(x, np.float32).astype(BF16)


def f32(x):
    return np.asarray(x, np.float32)


def f64(x):
    return np.asarray(x).astype(np.float64)


def striped(idx):
    return np.tile(idx.reshape(-1, 16).T, (8, 1))


H, S, N = 128, 512, 128
EPS = 1e-6


def setup_inputs():
    return {'table': bf(np.abs(np.random.standard_normal((H, S)))), 'a': bf(np.abs(np.random.standard_normal((H, N)))), 'w': bf(np.random.standard_normal((H, H)) / np.sqrt(H)), 'b3': f32(0.1 * np.random.standard_normal((H, 1))), 'h_e': f32(np.random.standard_normal((H, N))), 'gain': f32(1.0 + 0.1 * np.random.standard_normal((H, 1))), 'bias': f32(0.1 * np.random.standard_normal((H, 1))), 'offs': striped(np.random.permutation(S)[:N])}


def reference(table, a, w, b3, h_e, gain, bias, offs):
    idx = offs[:16].T.reshape(-1)
    fwd = f64(w).T @ f64(a) + f64(b3)
    rev = f64(w).T @ f64(table)[:, idx] + f64(b3)
    x = f64(h_e) + 0.5 * (fwd + rev)
    mu = x.mean(axis=0, keepdims=True)
    sigma = np.sqrt(((x - mu) ** 2).sum(axis=0, keepdims=True) / (H - 1))
    return f64(gain) * (x - mu) / (sigma + EPS) + f64(bias)

@@ -1,0 +1,81 @@
+import concourse.mybir as mybir
+
+H = 128
+S = 512
+N = 128
+EPS = 1e-6
+
+FLOPS = 2 * (2 * H * H * N)
+
+BF16, F32, U16 = mybir.dt.bfloat16, mybir.dt.float32, mybir.dt.uint16
+ALU = mybir.AluOpType
+ACT = mybir.ActivationFunctionType
+
+
+def tile_termedgempnnlayer_kernel(tc, table, a, w, b3, h_e, gain, bias, offs, out):
+    nc = tc.nc
+    with (
+        tc.tile_pool(name="held", bufs=1) as held,
+        tc.psum_pool(name="psum", bufs=1) as psum,
+    ):
+        offsets = held.tile([H, N // 16], U16, name="offsets")
+        nc.sync.dma_start(offsets[:], offs)
+        store = held.tile([H, S], BF16, name="store")
+        nc.sync.dma_start(store[:], table)
+        weights = held.tile([H, H], BF16, name="weights")
+        nc.scalar.dma_start(weights[:], w)
+        own = held.tile([H, N], BF16, name="own")
+        nc.scalar.dma_start(own[:], a)
+        state = held.tile([H, N], F32, name="state")
+        nc.sync.dma_start(state[:], h_e)
+        b3_col = held.tile([H, 1], F32, name="b3_col")
+        nc.scalar.dma_start(b3_col[:], b3)
+        gain_col = held.tile([H, 1], F32, name="gain_col")
+        nc.scalar.dma_start(gain_col[:], gain)
+        bias_col = held.tile([H, 1], F32, name="bias_col")
+        nc.scalar.dma_start(bias_col[:], bias)
+
+        centre = held.tile([H, H], F32, name="centre")
+        nc.gpsimd.memset(centre[:], -1.0 / H)
+        nc.gpsimd.affine_select(
+            out=centre[:],
+            in_=centre[:],
+            pattern=[[-1, H]],
+            compare_op=ALU.not_equal,
+            fill=1.0 - 1.0 / H,
+            base=0,
+            channel_multiplier=1,
+        )
+        ones = held.tile([H, H], F32, name="ones")
+        nc.vector.memset(ones[:], 1.0)
+
+        state_b3 = held.tile([H, N], F32, name="state_b3")
+        nc.vector.tensor_scalar_add(state_b3[:], state[:], b3_col[:])
+
+        messages = psum.tile([H, N], F32, name="messages")
+        nc.tensor.matmul(messages[:], weights[:], own[:], start=True, stop=False)
+        nc.tensor.matmul(messages[:], weights[:], store[:].indirect(offsets[:]), start=False, stop=True)
+
+        x = held.tile([H, N], F32, name="x")
+        nc.vector.scalar_tensor_tensor(x[:], messages[:], 0.5, state_b3[:], ALU.mult, ALU.add)
+
+        centred = psum.tile([H, N], F32, name="centred")
+        nc.tensor.matmul(centred[:], centre[:], x[:], start=True, stop=True)
+
+        squares = held.tile([H, N], F32, name="squares")
+        nc.scalar.activation(squares[:], centred[:], ACT.Square)
+        sum_sq = psum.tile([H, N], F32, name="sum_sq")
+        nc.tensor.matmul(sum_sq[:], ones[:], squares[:], start=True, stop=True)
+
+        sigma = held.tile([H, N], F32, name="sigma")
+        nc.scalar.activation(sigma[:], sum_sq[:], ACT.Sqrt, scale=1.0 / (H - 1))
+        sigma_eps = held.tile([H, N], F32, name="sigma_eps")
+        nc.vector.tensor_scalar_add(sigma_eps[:], sigma[:], EPS)
+        inverse = held.tile([H, N], F32, name="inverse")
+        nc.vector.reciprocal(inverse[:], sigma_eps[:])
+
+        scaled = held.tile([H, N], F32, name="scaled")
+        nc.vector.scalar_tensor_tensor(scaled[:], centred[:], gain_col[:], inverse[:], ALU.mult, ALU.mult)
+        result = held.tile([H, N], F32, name="result")
+        nc.vector.tensor_scalar_add(result[:], scaled[:], bias_col[:])
+        nc.sync.dma_start(out, result[:])

@@ -49,6 +49,11 @@ def tile_termedgempnnlayer_kernel(tc, table, a, w, b3, h_e, gain, bias, offs, ou
         ones = held.tile([H, H], F32, name="ones")
         nc.vector.memset(ones[:], 1.0)
 
+        scratch = held.tile([H, 1], F32, name="scratch")
+        nc.vector.memset(scratch[:], 1.0)
+        scratch_root = held.tile([H, 1], F32, name="scratch_root")
+        nc.scalar.activation(scratch_root[:], scratch[:], ACT.Sqrt)
+
         state_b3 = held.tile([H, N], F32, name="state_b3")
         nc.vector.tensor_scalar_add(state_b3[:], state[:], b3_col[:])
 

@@ -1,4 +1,5 @@
 import concourse.mybir as mybir
+from concourse.masks import make_identity
 
 H = 128
 S = 512
@@ -46,8 +47,8 @@ def tile_termedgempnnlayer_kernel(tc, table, a, w, b3, h_e, gain, bias, offs, ou
             base=0,
             channel_multiplier=1,
         )
-        ones = held.tile([H, H], F32, name="ones")
-        nc.vector.memset(ones[:], 1.0)
+        identity = held.tile([N, N], F32, name="identity")
+        make_identity(nc, identity[:])
 
         scratch = held.tile([H, 1], F32, name="scratch")
         nc.vector.memset(scratch[:], 1.0)
@@ -64,23 +65,25 @@ def tile_termedgempnnlayer_kernel(tc, table, a, w, b3, h_e, gain, bias, offs, ou
         x = held.tile([H, N], F32, name="x")
         nc.vector.scalar_tensor_tensor(x[:], messages[:], 0.5, state_b3[:], ALU.mult, ALU.add)
 
-        centred = psum.tile([H, N], F32, name="centred")
-        nc.tensor.matmul(centred[:], centre[:], x[:], start=True, stop=True)
+        centred_t = psum.tile([N, H], F32, name="centred_t")
+        nc.tensor.matmul(centred_t[:], x[:], centre[:], start=True, stop=True)
 
-        squares = held.tile([H, N], F32, name="squares")
-        nc.scalar.activation(squares[:], centred[:], ACT.Square)
-        sum_sq = psum.tile([H, N], F32, name="sum_sq")
-        nc.tensor.matmul(sum_sq[:], ones[:], squares[:], start=True, stop=True)
+        squares = held.tile([N, H], F32, name="squares")
+        sum_sq = held.tile([N, 1], F32, name="sum_sq")
+        nc.scalar.activation(squares[:], centred_t[:], ACT.Square, accum_out=sum_sq[:])
 
-        sigma = held.tile([H, N], F32, name="sigma")
+        sigma = held.tile([N, 1], F32, name="sigma")
         nc.scalar.activation(sigma[:], sum_sq[:], ACT.Sqrt, scale=1.0 / (H - 1))
-        sigma_eps = held.tile([H, N], F32, name="sigma_eps")
+        sigma_eps = held.tile([N, 1], F32, name="sigma_eps")
         nc.vector.tensor_scalar_add(sigma_eps[:], sigma[:], EPS)
-        inverse = held.tile([H, N], F32, name="inverse")
+        inverse = held.tile([N, 1], F32, name="inverse")
         nc.vector.reciprocal(inverse[:], sigma_eps[:])
 
-        scaled = held.tile([H, N], F32, name="scaled")
-        nc.vector.scalar_tensor_tensor(scaled[:], centred[:], gain_col[:], inverse[:], ALU.mult, ALU.mult)
+        normed_t = held.tile([N, H], F32, name="normed_t")
+        nc.vector.tensor_scalar_mul(normed_t[:], centred_t[:], inverse[:])
+        normed = psum.tile([H, N], F32, name="normed")
+        nc.tensor.transpose(normed[:], normed_t[:], identity[:])
+
         result = held.tile([H, N], F32, name="result")
-        nc.vector.tensor_scalar_add(result[:], scaled[:], bias_col[:])
+        nc.vector.tensor_scalar(result[:], normed[:], gain_col[:], bias_col[:], ALU.mult, ALU.add)
         nc.sync.dma_start(out, result[:])

@@ -5,6 +5,7 @@ H = 128
 S = 512
 N = 128
 EPS = 1e-6
+WARM_UP_MATMULS = 5
 
 FLOPS = 2 * (2 * H * H * N)
 
@@ -54,6 +55,12 @@ def tile_termedgempnnlayer_kernel(tc, table, a, w, b3, h_e, gain, bias, offs, ou
         nc.vector.memset(scratch[:], 1.0)
         scratch_root = held.tile([H, 1], F32, name="scratch_root")
         nc.scalar.activation(scratch_root[:], scratch[:], ACT.Sqrt)
+
+        zeros = held.tile([H, S], BF16, name="zeros")
+        nc.vector.memset(zeros[:], 0.0)
+        unused = psum.tile([H, S], F32, name="unused")
+        for _ in range(WARM_UP_MATMULS):
+            nc.tensor.matmul(unused[:], zeros[:, 0:H], zeros[:], start=True, stop=True)
 
         state_b3 = held.tile([H, N], F32, name="state_b3")
         nc.vector.tensor_scalar_add(state_b3[:], state[:], b3_col[:])

@@ -5,7 +5,7 @@ H = 128
 S = 512
 N = 128
 EPS = 1e-6
-WARM_UP_MATMULS = 5
+WARM_UP_MATMULS = 18
 
 FLOPS = 2 * (2 * H * H * N)
 
@@ -37,6 +37,12 @@ def tile_termedgempnnlayer_kernel(tc, table, a, w, b3, h_e, gain, bias, offs, ou
         bias_col = held.tile([H, 1], F32, name="bias_col")
         nc.scalar.dma_start(bias_col[:], bias)
 
+        zeros = held.tile([H, H], BF16, name="zeros")
+        nc.gpsimd.memset(zeros[:], 0.0)
+        unused = psum.tile([H, H], F32, name="unused")
+        for _ in range(WARM_UP_MATMULS):
+            nc.tensor.matmul(unused[:], zeros[:], zeros[:], start=True, stop=True)
+
         centre = held.tile([H, H], F32, name="centre")
         nc.gpsimd.memset(centre[:], -1.0 / H)
         nc.gpsimd.affine_select(
@@ -55,12 +61,6 @@ def tile_termedgempnnlayer_kernel(tc, table, a, w, b3, h_e, gain, bias, offs, ou
         nc.vector.memset(scratch[:], 1.0)
         scratch_root = held.tile([H, 1], F32, name="scratch_root")
         nc.scalar.activation(scratch_root[:], scratch[:], ACT.Sqrt)
-
-        zeros = held.tile([H, S], BF16, name="zeros")
-        nc.vector.memset(zeros[:], 0.0)
-        unused = psum.tile([H, S], F32, name="unused")
-        for _ in range(WARM_UP_MATMULS):
-            nc.tensor.matmul(unused[:], zeros[:, 0:H], zeros[:], start=True, stop=True)
 
         state_b3 = held.tile([H, N], F32, name="state_b3")
         nc.vector.tensor_scalar_add(state_b3[:], state[:], b3_col[:])

@@ -62,6 +62,9 @@ def tile_termedgempnnlayer_kernel(tc, table, a, w, b3, h_e, gain, bias, offs, ou
         scratch_root = held.tile([H, 1], F32, name="scratch_root")
         nc.scalar.activation(scratch_root[:], scratch[:], ACT.Sqrt)
 
+        radicands = held.tile([N, 2], F32, name="radicands")
+        nc.vector.memset(radicands[:], (H - 1) * EPS * EPS)
+
         state_b3 = held.tile([H, N], F32, name="state_b3")
         nc.vector.tensor_scalar_add(state_b3[:], state[:], b3_col[:])
 
@@ -76,13 +79,11 @@ def tile_termedgempnnlayer_kernel(tc, table, a, w, b3, h_e, gain, bias, offs, ou
         nc.tensor.matmul(centred_t[:], x[:], centre[:], start=True, stop=True)
 
         squares = held.tile([N, H], F32, name="squares")
-        sum_sq = held.tile([N, 1], F32, name="sum_sq")
-        nc.scalar.activation(squares[:], centred_t[:], ACT.Square, accum_out=sum_sq[:])
+        nc.scalar.activation(squares[:], centred_t[:], ACT.Square, accum_out=radicands[:, 0:1])
 
-        sigma = held.tile([N, 1], F32, name="sigma")
-        nc.scalar.activation(sigma[:], sum_sq[:], ACT.Sqrt, scale=1.0 / (H - 1))
+        roots = held.tile([N, 2], F32, name="roots")
         sigma_eps = held.tile([N, 1], F32, name="sigma_eps")
-        nc.vector.tensor_scalar_add(sigma_eps[:], sigma[:], EPS)
+        nc.scalar.activation(roots[:], radicands[:], ACT.Sqrt, scale=1.0 / (H - 1), accum_out=sigma_eps[:])
         inverse = held.tile([N, 1], F32, name="inverse")
         nc.vector.reciprocal(inverse[:], sigma_eps[:])
 

@@ -77,9 +77,13 @@ def tile_termedgempnnlayer_kernel(tc, table, a, w, b3, h_e, gain, bias, offs, ou
 
         centred_t = psum.tile([N, H], F32, name="centred_t")
         nc.tensor.matmul(centred_t[:], x[:], centre[:], start=True, stop=True)
+        centred = psum.tile([H, N], F32, name="centred")
+        nc.tensor.matmul(centred[:], centre[:], x[:], start=True, stop=True)
 
         squares = held.tile([N, H], F32, name="squares")
         nc.scalar.activation(squares[:], centred_t[:], ACT.Square, accum_out=radicands[:, 0:1])
+        scaled = held.tile([H, N], F32, name="scaled")
+        nc.vector.tensor_scalar_mul(scaled[:], centred[:], gain_col[:])
 
         roots = held.tile([N, 2], F32, name="roots")
         sigma_eps = held.tile([N, 1], F32, name="sigma_eps")
@@ -87,11 +91,13 @@ def tile_termedgempnnlayer_kernel(tc, table, a, w, b3, h_e, gain, bias, offs, ou
         inverse = held.tile([N, 1], F32, name="inverse")
         nc.vector.reciprocal(inverse[:], sigma_eps[:])
 
-        normed_t = held.tile([N, H], F32, name="normed_t")
-        nc.vector.tensor_scalar_mul(normed_t[:], centred_t[:], inverse[:])
-        normed = psum.tile([H, N], F32, name="normed")
-        nc.tensor.transpose(normed[:], normed_t[:], identity[:])
+        sigma_eps_rows = psum.tile([H, N], F32, name="sigma_eps_rows")
+        nc.tensor.transpose(sigma_eps_rows[:], sigma_eps[:].to_broadcast([N, H]), identity[:])
+        inverse_rows = psum.tile([H, N], F32, name="inverse_rows")
+        nc.tensor.transpose(inverse_rows[:], inverse[:].to_broadcast([N, H]), identity[:])
 
+        numerator = held.tile([H, N], F32, name="numerator")
+        nc.vector.scalar_tensor_tensor(numerator[:], sigma_eps_rows[:], bias_col[:], scaled[:], ALU.mult, ALU.add)
         result = held.tile([H, N], F32, name="result")
-        nc.vector.tensor_scalar(result[:], normed[:], gain_col[:], bias_col[:], ALU.mult, ALU.add)
+        nc.vector.tensor_tensor(result[:], numerator[:], inverse_rows[:], ALU.mult)
         nc.sync.dma_start(out, result[:])

@@ -28,14 +28,14 @@ def tile_termedgempnnlayer_kernel(tc, table, a, w, b3, h_e, gain, bias, offs, ou
         nc.scalar.dma_start(weights[:], w)
         own = held.tile([H, N], BF16, name="own")
         nc.scalar.dma_start(own[:], a)
+        b3_col = held.tile([H, 1], F32, name="b3_col")
+        nc.sync.dma_start(b3_col[:], b3)
         state = held.tile([H, N], F32, name="state")
         nc.sync.dma_start(state[:], h_e)
-        b3_col = held.tile([H, 1], F32, name="b3_col")
-        nc.scalar.dma_start(b3_col[:], b3)
         gain_col = held.tile([H, 1], F32, name="gain_col")
-        nc.scalar.dma_start(gain_col[:], gain)
+        nc.sync.dma_start(gain_col[:], gain)
         bias_col = held.tile([H, 1], F32, name="bias_col")
-        nc.scalar.dma_start(bias_col[:], bias)
+        nc.sync.dma_start(bias_col[:], bias)
 
         zeros = held.tile([H, H], BF16, name="zeros")
         nc.gpsimd.memset(zeros[:], 0.0)
@@ -43,19 +43,10 @@ def tile_termedgempnnlayer_kernel(tc, table, a, w, b3, h_e, gain, bias, offs, ou
         for _ in range(WARM_UP_MATMULS):
             nc.tensor.matmul(unused[:], zeros[:], zeros[:], start=True, stop=True)
 
-        centre = held.tile([H, H], F32, name="centre")
-        nc.gpsimd.memset(centre[:], -1.0 / H)
-        nc.gpsimd.affine_select(
-            out=centre[:],
-            in_=centre[:],
-            pattern=[[-1, H]],
-            compare_op=ALU.not_equal,
-            fill=1.0 - 1.0 / H,
-            base=0,
-            channel_multiplier=1,
-        )
         identity = held.tile([N, N], F32, name="identity")
         make_identity(nc, identity[:])
+        centre = held.tile([H, H], F32, name="centre")
+        nc.vector.tensor_scalar_add(centre[:], identity[:], -1.0 / H)
 
         scratch = held.tile([H, 1], F32, name="scratch")
         nc.vector.memset(scratch[:], 1.0)

@@ -5,7 +5,7 @@ H = 128
 S = 512
 N = 128
 EPS = 1e-6
-WARM_UP_MATMULS = 18
+WARM_UP_MATMULS = 16
 
 FLOPS = 2 * (2 * H * H * N)
 
@@ -20,10 +20,10 @@ def tile_termedgempnnlayer_kernel(tc, table, a, w, b3, h_e, gain, bias, offs, ou
         tc.tile_pool(name="held", bufs=1) as held,
         tc.psum_pool(name="psum", bufs=1) as psum,
     ):
-        offsets = held.tile([H, N // 16], U16, name="offsets")
-        nc.sync.dma_start(offsets[:], offs)
         store = held.tile([H, S], BF16, name="store")
         nc.sync.dma_start(store[:], table)
+        offsets = held.tile([H, N // 16], U16, name="offsets")
+        nc.sync.dma_start(offsets[:], offs)
         weights = held.tile([H, H], BF16, name="weights")
         nc.scalar.dma_start(weights[:], w)
         own = held.tile([H, N], BF16, name="own")

@@ -22,16 +22,16 @@ def tile_termedgempnnlayer_kernel(tc, table, a, w, b3, h_e, gain, bias, offs, ou
     ):
         store = held.tile([H, S], BF16, name="store")
         nc.sync.dma_start(store[:], table)
+        b3_col = held.tile([H, 1], F32, name="b3_col")
+        nc.scalar.dma_start(b3_col[:], b3)
         offsets = held.tile([H, N // 16], U16, name="offsets")
         nc.sync.dma_start(offsets[:], offs)
         weights = held.tile([H, H], BF16, name="weights")
         nc.scalar.dma_start(weights[:], w)
-        own = held.tile([H, N], BF16, name="own")
-        nc.scalar.dma_start(own[:], a)
-        b3_col = held.tile([H, 1], F32, name="b3_col")
-        nc.sync.dma_start(b3_col[:], b3)
         state = held.tile([H, N], F32, name="state")
         nc.sync.dma_start(state[:], h_e)
+        own = held.tile([H, N], BF16, name="own")
+        nc.scalar.dma_start(own[:], a)
         gain_col = held.tile([H, 1], F32, name="gain_col")
         nc.sync.dma_start(gain_col[:], gain)
         bias_col = held.tile([H, 1], F32, name="bias_col")

import concourse.mybir as mybir
from concourse.masks import make_identity

H = 128
S = 512
N = 128
EPS = 1e-6
WARM_UP_MATMULS = 16

FLOPS = 2 * (2 * H * H * N)

BF16, F32, U16 = mybir.dt.bfloat16, mybir.dt.float32, mybir.dt.uint16
ALU = mybir.AluOpType
ACT = mybir.ActivationFunctionType


def tile_termedgempnnlayer_kernel(tc, table, a, w, b3, h_e, gain, bias, offs, out):
    nc = tc.nc
    with (
        tc.tile_pool(name="held", bufs=1) as held,
        tc.psum_pool(name="psum", bufs=1) as psum,
    ):
        store = held.tile([H, S], BF16, name="store")
        nc.sync.dma_start(store[:], table)
        b3_col = held.tile([H, 1], F32, name="b3_col")
        nc.scalar.dma_start(b3_col[:], b3)
        offsets = held.tile([H, N // 16], U16, name="offsets")
        nc.sync.dma_start(offsets[:], offs)
        weights = held.tile([H, H], BF16, name="weights")
        nc.scalar.dma_start(weights[:], w)
        state = held.tile([H, N], F32, name="state")
        nc.sync.dma_start(state[:], h_e)
        own = held.tile([H, N], BF16, name="own")
        nc.scalar.dma_start(own[:], a)
        gain_col = held.tile([H, 1], F32, name="gain_col")
        nc.sync.dma_start(gain_col[:], gain)
        bias_col = held.tile([H, 1], F32, name="bias_col")
        nc.sync.dma_start(bias_col[:], bias)

        zeros = held.tile([H, H], BF16, name="zeros")
        nc.gpsimd.memset(zeros[:], 0.0)
        unused = psum.tile([H, H], F32, name="unused")
        for _ in range(WARM_UP_MATMULS):
            nc.tensor.matmul(unused[:], zeros[:], zeros[:], start=True, stop=True)

        identity = held.tile([N, N], F32, name="identity")
        make_identity(nc, identity[:])
        centre = held.tile([H, H], F32, name="centre")
        nc.vector.tensor_scalar_add(centre[:], identity[:], -1.0 / H)

        scratch = held.tile([H, 1], F32, name="scratch")
        nc.vector.memset(scratch[:], 1.0)
        scratch_root = held.tile([H, 1], F32, name="scratch_root")
        nc.scalar.activation(scratch_root[:], scratch[:], ACT.Sqrt)

        radicands = held.tile([N, 2], F32, name="radicands")
        nc.vector.memset(radicands[:], (H - 1) * EPS * EPS)

        state_b3 = held.tile([H, N], F32, name="state_b3")
        nc.vector.tensor_scalar_add(state_b3[:], state[:], b3_col[:])

        messages = psum.tile([H, N], F32, name="messages")
        nc.tensor.matmul(messages[:], weights[:], own[:], start=True, stop=False)
        nc.tensor.matmul(messages[:], weights[:], store[:].indirect(offsets[:]), start=False, stop=True)

        x = held.tile([H, N], F32, name="x")
        nc.vector.scalar_tensor_tensor(x[:], messages[:], 0.5, state_b3[:], ALU.mult, ALU.add)

        centred_t = psum.tile([N, H], F32, name="centred_t")
        nc.tensor.matmul(centred_t[:], x[:], centre[:], start=True, stop=True)
        centred = psum.tile([H, N], F32, name="centred")
        nc.tensor.matmul(centred[:], centre[:], x[:], start=True, stop=True)

        squares = held.tile([N, H], F32, name="squares")
        nc.scalar.activation(squares[:], centred_t[:], ACT.Square, accum_out=radicands[:, 0:1])
        scaled = held.tile([H, N], F32, name="scaled")
        nc.vector.tensor_scalar_mul(scaled[:], centred[:], gain_col[:])

        roots = held.tile([N, 2], F32, name="roots")
        sigma_eps = held.tile([N, 1], F32, name="sigma_eps")
        nc.scalar.activation(roots[:], radicands[:], ACT.Sqrt, scale=1.0 / (H - 1), accum_out=sigma_eps[:])
        inverse = held.tile([N, 1], F32, name="inverse")
        nc.vector.reciprocal(inverse[:], sigma_eps[:])

        sigma_eps_rows = psum.tile([H, N], F32, name="sigma_eps_rows")
        nc.tensor.transpose(sigma_eps_rows[:], sigma_eps[:].to_broadcast([N, H]), identity[:])
        inverse_rows = psum.tile([H, N], F32, name="inverse_rows")
        nc.tensor.transpose(inverse_rows[:], inverse[:].to_broadcast([N, H]), identity[:])

        numerator = held.tile([H, N], F32, name="numerator")
        nc.vector.scalar_tensor_tensor(numerator[:], sigma_eps_rows[:], bias_col[:], scaled[:], ALU.mult, ALU.add)
        result = held.tile([H, N], F32, name="result")
        nc.vector.tensor_tensor(result[:], numerator[:], inverse_rows[:], ALU.mult)
        nc.sync.dma_start(out, result[:])
